import numpy as np
import ml_dtypes

BF16 = ml_dtypes.bfloat16


def bf(x):
    return np.asarray(x, np.float32).astype(BF16)


def f32(x):
    return np.asarray(x, np.float32)


def f64(x):
    return np.asarray(x).astype(np.float64)


def striped(idx):
    return np.tile(idx.reshape(-1, 16).T, (8, 1))


C, S, N, G, K = 128, 256, 128, 16, 3
RES = 0.5
DIM = 23.5
CENTER = DIM / 2.0 - (G - 1) * RES / 2.0
ORIGIN = CENTER - DIM / 2.0


def density(coords, radii):
    ax = ORIGIN + RES * np.arange(G)
    dx2 = (ax[None, :] - coords[:, 0:1]) ** 2
    dy2 = (ax[None, :] - coords[:, 1:2]) ** 2
    dz2 = (ax[None, :] - coords[:, 2:3]) ** 2
    d2 = (dx2[:, :, None, None] + dy2[:, None, :, None] + dz2[:, None, None, :]).reshape(C, G * G * G)
    q = d2 / (radii * radii)
    u = np.sqrt(q)
    return np.where(u < 1.0, np.exp(-2.0 * q), np.where(u < 1.5, np.exp(-2.0) * (4.0 * q - 12.0 * u + 9.0), 0.0))


def setup_inputs():
    return {"coords": f32(2.5 * np.random.standard_normal((C, K))), "radii": f32(1.0 + 0.8 * np.random.uniform(size=(C, 1))), "types": f32(bf(np.random.uniform(size=(C, S)))), "offs": striped(np.random.permutation(S)[:N])}


def reference(coords, radii, types, offs):
    idx = offs[:16].T.reshape(-1)
    dens = density(f64(coords), f64(radii))
    return f64(types)[:, idx].T @ dens

@@ -1,0 +1,120 @@
+import math
+
+import concourse.mybir as mybir
+
+F32 = mybir.dt.float32
+BF16 = mybir.dt.bfloat16
+U16 = mybir.dt.uint16
+ALU = mybir.AluOpType
+FN = mybir.ActivationFunctionType
+
+ATOMS = 128
+CHANNELS = 256
+PICKED = 128
+G = 16
+SLAB = G * G
+POINTS = G * SLAB
+BANK = 512
+SLABS_IN_BANK = BANK // SLAB
+
+GRID_ORIGIN = -3.75
+GRID_STEP = 0.5
+Q_CORE = 1.0
+Q_END = 2.25
+GAUSS_AT_CORE = math.exp(-2.0 * Q_CORE)
+
+FLOPS = 2 * ATOMS * PICKED * POINTS
+
+
+def tile_coords2grid_kernel(tc, coords, radii, types, offs, out):
+    nc = tc.nc
+    with (
+        tc.tile_pool(name="held", bufs=1) as held,
+        tc.tile_pool(name="work", bufs=3) as work,
+        tc.psum_pool(name="psum", bufs=4) as psum,
+    ):
+        xyz = held.tile([ATOMS, 3], F32)
+        nc.sync.dma_start(xyz[:], coords)
+        radius = held.tile([ATOMS, 1], F32)
+        nc.sync.dma_start(radius[:], radii)
+        offsets = held.tile([ATOMS, PICKED // 16], U16)
+        nc.sync.dma_start(offsets[:], offs)
+        table = held.tile([ATOMS, CHANNELS], F32)
+        nc.sync.dma_start(table[:], types)
+
+        picked = held.tile([ATOMS, PICKED], F32)
+        nc.scalar.activation(picked[:], table[:].indirect(offsets[:]), FN.Copy)
+        weights = held.tile([ATOMS, PICKED], BF16)
+        nc.gpsimd.tensor_copy(weights[:], picked[:])
+
+        steps = held.tile([ATOMS, 3, G], F32)
+        nc.gpsimd.iota(
+            steps[:],
+            pattern=[[0, 3], [1, G]],
+            base=0,
+            channel_multiplier=0,
+            allow_small_or_imprecise_dtypes=True,
+        )
+        axis = held.tile([ATOMS, 3, G], F32)
+        nc.gpsimd.tensor_scalar(axis[:], steps[:], GRID_STEP, GRID_ORIGIN, ALU.mult, ALU.add)
+        three = held.tile([ATOMS, 1], F32)
+        nc.gpsimd.memset(three[:], 3.0)
+
+        radius_sq = held.tile([ATOMS, 1], F32)
+        nc.vector.tensor_tensor(radius_sq[:], radius[:], radius[:], ALU.mult)
+        inv_radius_sq = held.tile([ATOMS, 1], F32)
+        nc.vector.reciprocal(inv_radius_sq[:], radius_sq[:])
+        delta = held.tile([ATOMS, 3, G], F32)
+        nc.vector.tensor_tensor(
+            delta[:], axis[:], xyz[:].unsqueeze(2).to_broadcast([ATOMS, 3, G]), ALU.subtract
+        )
+        q_far = held.tile([ATOMS, 3, G], F32)
+        nc.vector.scalar_tensor_tensor(
+            q_far[:], delta[:], inv_radius_sq[:], delta[:], op0=ALU.mult, op1=ALU.mult
+        )
+        q_axis = held.tile([ATOMS, 3, G], F32)
+        nc.vector.tensor_scalar_min(q_axis[:], q_far[:], Q_END)
+        q_x = q_axis[:, 0, :]
+
+        q_yz = held.tile([ATOMS, SLAB], F32)
+        nc.vector.tensor_tensor(
+            q_yz[:].rearrange("n (y z) -> n y z", y=G),
+            q_axis[:, 1, :].unsqueeze(2).to_broadcast([ATOMS, G, G]),
+            q_axis[:, 2, :].unsqueeze(1).to_broadcast([ATOMS, G, G]),
+            ALU.add,
+        )
+        low = held.tile([ATOMS, G], F32)
+        nc.vector.tensor_scalar(low[:], q_x, -1.0, Q_CORE, ALU.mult, ALU.add)
+        high = held.tile([ATOMS, G], F32)
+        nc.vector.tensor_scalar(high[:], q_x, -1.0, Q_END, ALU.mult, ALU.add)
+        gauss_x = held.tile([ATOMS, G], F32)
+        nc.scalar.activation(gauss_x[:], q_x, FN.Exp, scale=-2.0)
+        gauss_yz = held.tile([ATOMS, SLAB], F32)
+        nc.scalar.activation(gauss_yz[:], q_yz[:], FN.Exp, scale=-2.0)
+
+        for bank in range(POINTS // BANK):
+            q_clamped = work.tile([ATOMS, BANK], F32)
+            u_clamped = work.tile([ATOMS, BANK], F32)
+            core = work.tile([ATOMS, BANK], F32)
+            for s in range(SLABS_IN_BANK):
+                gx = bank * SLABS_IN_BANK + s
+                cols = slice(s * SLAB, (s + 1) * SLAB)
+                nc.vector.tensor_scalar(
+                    q_clamped[:, cols], q_yz[:], low[:, gx : gx + 1], high[:, gx : gx + 1], ALU.max, ALU.min
+                )
+                nc.scalar.activation(
+                    u_clamped[:, cols], q_clamped[:, cols], FN.Sqrt, bias=q_axis[:, 0, gx : gx + 1]
+                )
+                nc.vector.tensor_scalar(
+                    core[:, cols], gauss_yz[:], gauss_x[:, gx : gx + 1], GAUSS_AT_CORE, ALU.mult, ALU.max
+                )
+            tail = work.tile([ATOMS, BANK], F32)
+            nc.scalar.activation(tail[:], u_clamped[:], FN.Square, bias=three[:], scale=-2.0)
+            dens = work.tile([ATOMS, BANK], BF16)
+            nc.vector.tensor_tensor(dens[:], core[:], tail[:], ALU.mult)
+
+            acc = psum.tile([PICKED, BANK], F32)
+            nc.tensor.matmul(acc[:], weights[:], dens[:], start=True, stop=True)
+            staged = work.tile([PICKED, BANK], F32)
+            nc.vector.tensor_copy(staged[:], acc[:])
+            nc.sync.dma_start(out[:, bank * BANK : (bank + 1) * BANK], staged[:])

@@ -1,5 +1,3 @@
-import math
-
 import concourse.mybir as mybir
 
 F32 = mybir.dt.float32
@@ -15,13 +13,13 @@ G = 16
 SLAB = G * G
 POINTS = G * SLAB
 BANK = 512
+BANKS = POINTS // BANK
 SLABS_IN_BANK = BANK // SLAB
 
 GRID_ORIGIN = -3.75
 GRID_STEP = 0.5
 Q_CORE = 1.0
 Q_END = 2.25
-GAUSS_AT_CORE = math.exp(-2.0 * Q_CORE)
 
 FLOPS = 2 * ATOMS * PICKED * POINTS
 
@@ -30,8 +28,7 @@ def tile_coords2grid_kernel(tc, coords, radii, types, offs, out):
     nc = tc.nc
     with (
         tc.tile_pool(name="held", bufs=1) as held,
-        tc.tile_pool(name="work", bufs=3) as work,
-        tc.psum_pool(name="psum", bufs=4) as psum,
+        tc.psum_pool(name="psum", bufs=1) as psum,
     ):
         xyz = held.tile([ATOMS, 3], F32)
         nc.sync.dma_start(xyz[:], coords)
@@ -41,11 +38,6 @@ def tile_coords2grid_kernel(tc, coords, radii, types, offs, out):
         nc.sync.dma_start(offsets[:], offs)
         table = held.tile([ATOMS, CHANNELS], F32)
         nc.sync.dma_start(table[:], types)
-
-        picked = held.tile([ATOMS, PICKED], F32)
-        nc.scalar.activation(picked[:], table[:].indirect(offsets[:]), FN.Copy)
-        weights = held.tile([ATOMS, PICKED], BF16)
-        nc.gpsimd.tensor_copy(weights[:], picked[:])
 
         steps = held.tile([ATOMS, 3, G], F32)
         nc.gpsimd.iota(
@@ -57,8 +49,16 @@ def tile_coords2grid_kernel(tc, coords, radii, types, offs, out):
         )
         axis = held.tile([ATOMS, 3, G], F32)
         nc.gpsimd.tensor_scalar(axis[:], steps[:], GRID_STEP, GRID_ORIGIN, ALU.mult, ALU.add)
-        three = held.tile([ATOMS, 1], F32)
-        nc.gpsimd.memset(three[:], 3.0)
+        minus_two = held.tile([ATOMS, 1], F32)
+        nc.gpsimd.memset(minus_two[:], -2.0)
+
+        warmed = held.tile([ATOMS, 1], F32)
+        nc.scalar.activation(warmed[:], minus_two[:], FN.Exp)
+
+        picked = held.tile([ATOMS, PICKED], F32)
+        nc.scalar.activation(picked[:], table[:].indirect(offsets[:]), FN.Copy)
+        weights = held.tile([ATOMS, PICKED], BF16)
+        nc.gpsimd.tensor_copy(weights[:], picked[:])
 
         radius_sq = held.tile([ATOMS, 1], F32)
         nc.vector.tensor_tensor(radius_sq[:], radius[:], radius[:], ALU.mult)
@@ -76,6 +76,13 @@ def tile_coords2grid_kernel(tc, coords, radii, types, offs, out):
         nc.vector.tensor_scalar_min(q_axis[:], q_far[:], Q_END)
         q_x = q_axis[:, 0, :]
 
+        gauss_axis = held.tile([ATOMS, 2, G], F32)
+        nc.scalar.activation(gauss_axis[:], q_axis[:, 1:3, :], FN.Exp, scale=-2.0)
+        root_x = held.tile([ATOMS, G], F32)
+        nc.scalar.activation(root_x[:], q_x, FN.Exp, scale=-1.0)
+        floor_x = held.tile([ATOMS, G], F32)
+        nc.scalar.activation(floor_x[:], q_x, FN.Exp, bias=minus_two[:], scale=2.0)
+
         q_yz = held.tile([ATOMS, SLAB], F32)
         nc.vector.tensor_tensor(
             q_yz[:].rearrange("n (y z) -> n y z", y=G),
@@ -87,34 +94,67 @@ def tile_coords2grid_kernel(tc, coords, radii, types, offs, out):
         nc.vector.tensor_scalar(low[:], q_x, -1.0, Q_CORE, ALU.mult, ALU.add)
         high = held.tile([ATOMS, G], F32)
         nc.vector.tensor_scalar(high[:], q_x, -1.0, Q_END, ALU.mult, ALU.add)
-        gauss_x = held.tile([ATOMS, G], F32)
-        nc.scalar.activation(gauss_x[:], q_x, FN.Exp, scale=-2.0)
+        tail_scale = held.tile([ATOMS, G], F32)
+        nc.vector.tensor_scalar_mul(tail_scale[:], root_x[:], -2.0)
+        tail_bias = held.tile([ATOMS, G], F32)
+        nc.vector.tensor_scalar_mul(tail_bias[:], root_x[:], 3.0)
         gauss_yz = held.tile([ATOMS, SLAB], F32)
-        nc.scalar.activation(gauss_yz[:], q_yz[:], FN.Exp, scale=-2.0)
+        nc.vector.tensor_tensor(
+            gauss_yz[:].rearrange("n (y z) -> n y z", y=G),
+            gauss_axis[:, 0, :].unsqueeze(2).to_broadcast([ATOMS, G, G]),
+            gauss_axis[:, 1, :].unsqueeze(1).to_broadcast([ATOMS, G, G]),
+            ALU.mult,
+        )
 
-        for bank in range(POINTS // BANK):
-            q_clamped = work.tile([ATOMS, BANK], F32)
-            u_clamped = work.tile([ATOMS, BANK], F32)
-            core = work.tile([ATOMS, BANK], F32)
-            for s in range(SLABS_IN_BANK):
-                gx = bank * SLABS_IN_BANK + s
-                cols = slice(s * SLAB, (s + 1) * SLAB)
-                nc.vector.tensor_scalar(
-                    q_clamped[:, cols], q_yz[:], low[:, gx : gx + 1], high[:, gx : gx + 1], ALU.max, ALU.min
-                )
+        q_clamped = held.tile([ATOMS, POINTS], F32)
+        u_clamped = held.tile([ATOMS, POINTS], F32)
+        tail = held.tile([ATOMS, POINTS], F32)
+        dens = held.tile([ATOMS, POINTS], BF16)
+        staged = held.tile([PICKED, POINTS], F32)
+        acc = [psum.tile([PICKED, BANK], F32, name=f"acc{b}") for b in range(BANKS)]
+
+        for gx in range(G):
+            slab = slice(gx * SLAB, (gx + 1) * SLAB)
+            nc.vector.tensor_scalar(
+                q_clamped[:, slab], q_yz[:], low[:, gx : gx + 1], high[:, gx : gx + 1], ALU.max, ALU.min
+            )
+
+        def copy_out(b):
+            bank = slice(b * BANK, (b + 1) * BANK)
+            if b == BANKS - 2:
+                nc.scalar.copy(staged[:, bank], acc[b][:])
+            else:
+                nc.vector.tensor_copy(staged[:, bank], acc[b][:])
+            nc.sync.dma_start(out[:, bank], staged[:, bank])
+
+        def roots(b):
+            for gx in range(b * SLABS_IN_BANK, (b + 1) * SLABS_IN_BANK):
+                slab = slice(gx * SLAB, (gx + 1) * SLAB)
                 nc.scalar.activation(
-                    u_clamped[:, cols], q_clamped[:, cols], FN.Sqrt, bias=q_axis[:, 0, gx : gx + 1]
+                    u_clamped[:, slab], q_clamped[:, slab], FN.Sqrt, bias=q_axis[:, 0, gx : gx + 1]
                 )
-                nc.vector.tensor_scalar(
-                    core[:, cols], gauss_yz[:], gauss_x[:, gx : gx + 1], GAUSS_AT_CORE, ALU.mult, ALU.max
-                )
-            tail = work.tile([ATOMS, BANK], F32)
-            nc.scalar.activation(tail[:], u_clamped[:], FN.Square, bias=three[:], scale=-2.0)
-            dens = work.tile([ATOMS, BANK], BF16)
-            nc.vector.tensor_tensor(dens[:], core[:], tail[:], ALU.mult)
 
-            acc = psum.tile([PICKED, BANK], F32)
-            nc.tensor.matmul(acc[:], weights[:], dens[:], start=True, stop=True)
-            staged = work.tile([PICKED, BANK], F32)
-            nc.vector.tensor_copy(staged[:], acc[:])
-            nc.sync.dma_start(out[:, bank * BANK : (bank + 1) * BANK], staged[:])
+        roots(0)
+        for b in range(BANKS):
+            slabs = range(b * SLABS_IN_BANK, (b + 1) * SLABS_IN_BANK)
+            if b + 1 < BANKS:
+                roots(b + 1)
+            for gx in slabs:
+                slab = slice(gx * SLAB, (gx + 1) * SLAB)
+                nc.scalar.activation(
+                    tail[:, slab],
+                    u_clamped[:, slab],
+                    FN.Square,
+                    bias=tail_bias[:, gx : gx + 1],
+                    scale=tail_scale[:, gx : gx + 1],
+                )
+            for gx in slabs:
+                slab = slice(gx * SLAB, (gx + 1) * SLAB)
+                nc.vector.scalar_tensor_tensor(
+                    dens[:, slab], gauss_yz[:], floor_x[:, gx : gx + 1], tail[:, slab], op0=ALU.max, op1=ALU.mult
+                )
+            bank = slice(b * BANK, (b + 1) * BANK)
+            nc.tensor.matmul(acc[b][:], weights[:], dens[:, bank], start=True, stop=True)
+            if b > 0:
+                copy_out(b - 1)
+        copy_out(BANKS - 1)

@@ -1,3 +1,5 @@
+import math
+
 import concourse.mybir as mybir
 
 F32 = mybir.dt.float32
@@ -12,32 +14,34 @@ PICKED = 128
 G = 16
 SLAB = G * G
 POINTS = G * SLAB
-BANK = 512
-BANKS = POINTS // BANK
-SLABS_IN_BANK = BANK // SLAB
+PSUM_BANKS = 8
 
 GRID_ORIGIN = -3.75
 GRID_STEP = 0.5
 Q_CORE = 1.0
 Q_END = 2.25
+GAUSS_AT_END = math.exp(-2.0 * Q_END)
 
 FLOPS = 2 * ATOMS * PICKED * POINTS
+
+ROOTS_AHEAD = 2
+COPY_BEHIND = 2
 
 
 def tile_coords2grid_kernel(tc, coords, radii, types, offs, out):
     nc = tc.nc
     with (
         tc.tile_pool(name="held", bufs=1) as held,
-        tc.psum_pool(name="psum", bufs=1) as psum,
+        tc.psum_pool(name="psum", bufs=PSUM_BANKS) as psum,
     ):
         xyz = held.tile([ATOMS, 3], F32)
         nc.sync.dma_start(xyz[:], coords)
         radius = held.tile([ATOMS, 1], F32)
-        nc.sync.dma_start(radius[:], radii)
+        nc.scalar.dma_start(radius[:], radii)
         offsets = held.tile([ATOMS, PICKED // 16], U16)
         nc.sync.dma_start(offsets[:], offs)
         table = held.tile([ATOMS, CHANNELS], F32)
-        nc.sync.dma_start(table[:], types)
+        nc.scalar.dma_start(table[:], types)
 
         steps = held.tile([ATOMS, 3, G], F32)
         nc.gpsimd.iota(
@@ -49,40 +53,34 @@ def tile_coords2grid_kernel(tc, coords, radii, types, offs, out):
         )
         axis = held.tile([ATOMS, 3, G], F32)
         nc.gpsimd.tensor_scalar(axis[:], steps[:], GRID_STEP, GRID_ORIGIN, ALU.mult, ALU.add)
-        minus_two = held.tile([ATOMS, 1], F32)
-        nc.gpsimd.memset(minus_two[:], -2.0)
 
-        warmed = held.tile([ATOMS, 1], F32)
-        nc.scalar.activation(warmed[:], minus_two[:], FN.Exp)
+        two = held.tile([ATOMS, 1], F32)
+        nc.vector.memset(two[:], 2.0)
+        inv_gauss_at_core = held.tile([ATOMS, 1], F32)
+        nc.scalar.activation(inv_gauss_at_core[:], two[:], FN.Exp, scale=Q_CORE)
+
+        inv_radius = held.tile([ATOMS, 1], F32)
+        nc.vector.reciprocal(inv_radius[:], radius[:])
+        delta = held.tile([ATOMS, 3, G], F32)
+        nc.vector.tensor_tensor(
+            delta[:], axis[:], xyz[:].unsqueeze(2).to_broadcast([ATOMS, 3, G]), ALU.subtract
+        )
+        q_far = held.tile([ATOMS, 3, G], F32)
+        nc.scalar.activation(q_far[:], delta[:], FN.Square, scale=inv_radius[:])
+
+        gauss_axis = held.tile([ATOMS, 3, G], F32)
+        nc.scalar.activation(gauss_axis[:], q_far[:], FN.Exp, scale=-2.0)
+        root_x = held.tile([ATOMS, G], F32)
+        nc.scalar.activation(root_x[:], q_far[:, 0, :], FN.Exp, scale=-1.0)
 
         picked = held.tile([ATOMS, PICKED], F32)
         nc.scalar.activation(picked[:], table[:].indirect(offsets[:]), FN.Copy)
         weights = held.tile([ATOMS, PICKED], BF16)
         nc.gpsimd.tensor_copy(weights[:], picked[:])
 
-        radius_sq = held.tile([ATOMS, 1], F32)
-        nc.vector.tensor_tensor(radius_sq[:], radius[:], radius[:], ALU.mult)
-        inv_radius_sq = held.tile([ATOMS, 1], F32)
-        nc.vector.reciprocal(inv_radius_sq[:], radius_sq[:])
-        delta = held.tile([ATOMS, 3, G], F32)
-        nc.vector.tensor_tensor(
-            delta[:], axis[:], xyz[:].unsqueeze(2).to_broadcast([ATOMS, 3, G]), ALU.subtract
-        )
-        q_far = held.tile([ATOMS, 3, G], F32)
-        nc.vector.scalar_tensor_tensor(
-            q_far[:], delta[:], inv_radius_sq[:], delta[:], op0=ALU.mult, op1=ALU.mult
-        )
         q_axis = held.tile([ATOMS, 3, G], F32)
         nc.vector.tensor_scalar_min(q_axis[:], q_far[:], Q_END)
         q_x = q_axis[:, 0, :]
-
-        gauss_axis = held.tile([ATOMS, 2, G], F32)
-        nc.scalar.activation(gauss_axis[:], q_axis[:, 1:3, :], FN.Exp, scale=-2.0)
-        root_x = held.tile([ATOMS, G], F32)
-        nc.scalar.activation(root_x[:], q_x, FN.Exp, scale=-1.0)
-        floor_x = held.tile([ATOMS, G], F32)
-        nc.scalar.activation(floor_x[:], q_x, FN.Exp, bias=minus_two[:], scale=2.0)
-
         q_yz = held.tile([ATOMS, SLAB], F32)
         nc.vector.tensor_tensor(
             q_yz[:].rearrange("n (y z) -> n y z", y=G),
@@ -94,67 +92,65 @@ def tile_coords2grid_kernel(tc, coords, radii, types, offs, out):
         nc.vector.tensor_scalar(low[:], q_x, -1.0, Q_CORE, ALU.mult, ALU.add)
         high = held.tile([ATOMS, G], F32)
         nc.vector.tensor_scalar(high[:], q_x, -1.0, Q_END, ALU.mult, ALU.add)
+
         tail_scale = held.tile([ATOMS, G], F32)
         nc.vector.tensor_scalar_mul(tail_scale[:], root_x[:], -2.0)
         tail_bias = held.tile([ATOMS, G], F32)
         nc.vector.tensor_scalar_mul(tail_bias[:], root_x[:], 3.0)
+        inv_floor_x = held.tile([ATOMS, G], F32)
+        nc.vector.tensor_scalar(
+            inv_floor_x[:], gauss_axis[:, 0, :], GAUSS_AT_END, inv_gauss_at_core[:], ALU.max, ALU.mult
+        )
         gauss_yz = held.tile([ATOMS, SLAB], F32)
         nc.vector.tensor_tensor(
             gauss_yz[:].rearrange("n (y z) -> n y z", y=G),
-            gauss_axis[:, 0, :].unsqueeze(2).to_broadcast([ATOMS, G, G]),
-            gauss_axis[:, 1, :].unsqueeze(1).to_broadcast([ATOMS, G, G]),
+            gauss_axis[:, 1, :].unsqueeze(2).to_broadcast([ATOMS, G, G]),
+            gauss_axis[:, 2, :].unsqueeze(1).to_broadcast([ATOMS, G, G]),
             ALU.mult,
         )
+        floor_x = held.tile([ATOMS, G], F32)
+        nc.vector.reciprocal(floor_x[:], inv_floor_x[:])
 
         q_clamped = held.tile([ATOMS, POINTS], F32)
         u_clamped = held.tile([ATOMS, POINTS], F32)
         tail = held.tile([ATOMS, POINTS], F32)
         dens = held.tile([ATOMS, POINTS], BF16)
         staged = held.tile([PICKED, POINTS], F32)
-        acc = [psum.tile([PICKED, BANK], F32, name=f"acc{b}") for b in range(BANKS)]
+        slabs = [slice(gx * SLAB, (gx + 1) * SLAB) for gx in range(G)]
+        sums = {}
 
         for gx in range(G):
-            slab = slice(gx * SLAB, (gx + 1) * SLAB)
             nc.vector.tensor_scalar(
-                q_clamped[:, slab], q_yz[:], low[:, gx : gx + 1], high[:, gx : gx + 1], ALU.max, ALU.min
+                q_clamped[:, slabs[gx]], q_yz[:], low[:, gx : gx + 1], high[:, gx : gx + 1], ALU.max, ALU.min
             )
 
-        def copy_out(b):
-            bank = slice(b * BANK, (b + 1) * BANK)
-            if b == BANKS - 2:
-                nc.scalar.copy(staged[:, bank], acc[b][:])
-            else:
-                nc.vector.tensor_copy(staged[:, bank], acc[b][:])
-            nc.sync.dma_start(out[:, bank], staged[:, bank])
+        def root(gx):
+            nc.scalar.activation(
+                u_clamped[:, slabs[gx]], q_clamped[:, slabs[gx]], FN.Sqrt, bias=q_axis[:, 0, gx : gx + 1]
+            )
 
-        def roots(b):
-            for gx in range(b * SLABS_IN_BANK, (b + 1) * SLABS_IN_BANK):
-                slab = slice(gx * SLAB, (gx + 1) * SLAB)
-                nc.scalar.activation(
-                    u_clamped[:, slab], q_clamped[:, slab], FN.Sqrt, bias=q_axis[:, 0, gx : gx + 1]
-                )
+        def copy_out(gx):
+            nc.vector.tensor_copy(staged[:, slabs[gx]], sums[gx][:])
+            nc.sync.dma_start(out[:, slabs[gx]], staged[:, slabs[gx]])
 
-        roots(0)
-        for b in range(BANKS):
-            slabs = range(b * SLABS_IN_BANK, (b + 1) * SLABS_IN_BANK)
-            if b + 1 < BANKS:
-                roots(b + 1)
-            for gx in slabs:
-                slab = slice(gx * SLAB, (gx + 1) * SLAB)
-                nc.scalar.activation(
-                    tail[:, slab],
-                    u_clamped[:, slab],
-                    FN.Square,
-                    bias=tail_bias[:, gx : gx + 1],
-                    scale=tail_scale[:, gx : gx + 1],
-                )
-            for gx in slabs:
-                slab = slice(gx * SLAB, (gx + 1) * SLAB)
-                nc.vector.scalar_tensor_tensor(
-                    dens[:, slab], gauss_yz[:], floor_x[:, gx : gx + 1], tail[:, slab], op0=ALU.max, op1=ALU.mult
-                )
-            bank = slice(b * BANK, (b + 1) * BANK)
-            nc.tensor.matmul(acc[b][:], weights[:], dens[:, bank], start=True, stop=True)
-            if b > 0:
-                copy_out(b - 1)
-        copy_out(BANKS - 1)
+        for gx in range(ROOTS_AHEAD):
+            root(gx)
+        for gx in range(G):
+            if gx + ROOTS_AHEAD < G:
+                root(gx + ROOTS_AHEAD)
+            nc.scalar.activation(
+                tail[:, slabs[gx]],
+                u_clamped[:, slabs[gx]],
+                FN.Square,
+                bias=tail_bias[:, gx : gx + 1],
+                scale=tail_scale[:, gx : gx + 1],
+            )
+            nc.vector.scalar_tensor_tensor(
+                dens[:, slabs[gx]], gauss_yz[:], floor_x[:, gx : gx + 1], tail[:, slabs[gx]], op0=ALU.max, op1=ALU.mult
+            )
+            sums[gx] = psum.tile([PICKED, SLAB], F32, name="sums")
+            nc.tensor.matmul(sums[gx][:], weights[:], dens[:, slabs[gx]], start=True, stop=True)
+            if gx >= COPY_BEHIND:
+                copy_out(gx - COPY_BEHIND)
+        for gx in range(G - COPY_BEHIND, G):
+            copy_out(gx)

@@ -24,9 +24,6 @@ GAUSS_AT_END = math.exp(-2.0 * Q_END)
 
 FLOPS = 2 * ATOMS * PICKED * POINTS
 
-ROOTS_AHEAD = 2
-COPY_BEHIND = 2
-
 
 def tile_coords2grid_kernel(tc, coords, radii, types, offs, out):
     nc = tc.nc
@@ -117,27 +114,14 @@ def tile_coords2grid_kernel(tc, coords, radii, types, offs, out):
         dens = held.tile([ATOMS, POINTS], BF16)
         staged = held.tile([PICKED, POINTS], F32)
         slabs = [slice(gx * SLAB, (gx + 1) * SLAB) for gx in range(G)]
-        sums = {}
 
         for gx in range(G):
             nc.vector.tensor_scalar(
                 q_clamped[:, slabs[gx]], q_yz[:], low[:, gx : gx + 1], high[:, gx : gx + 1], ALU.max, ALU.min
             )
-
-        def root(gx):
             nc.scalar.activation(
                 u_clamped[:, slabs[gx]], q_clamped[:, slabs[gx]], FN.Sqrt, bias=q_axis[:, 0, gx : gx + 1]
             )
-
-        def copy_out(gx):
-            nc.vector.tensor_copy(staged[:, slabs[gx]], sums[gx][:])
-            nc.sync.dma_start(out[:, slabs[gx]], staged[:, slabs[gx]])
-
-        for gx in range(ROOTS_AHEAD):
-            root(gx)
-        for gx in range(G):
-            if gx + ROOTS_AHEAD < G:
-                root(gx + ROOTS_AHEAD)
             nc.scalar.activation(
                 tail[:, slabs[gx]],
                 u_clamped[:, slabs[gx]],
@@ -148,9 +132,7 @@ def tile_coords2grid_kernel(tc, coords, radii, types, offs, out):
             nc.vector.scalar_tensor_tensor(
                 dens[:, slabs[gx]], gauss_yz[:], floor_x[:, gx : gx + 1], tail[:, slabs[gx]], op0=ALU.max, op1=ALU.mult
             )
-            sums[gx] = psum.tile([PICKED, SLAB], F32, name="sums")
-            nc.tensor.matmul(sums[gx][:], weights[:], dens[:, slabs[gx]], start=True, stop=True)
-            if gx >= COPY_BEHIND:
-                copy_out(gx - COPY_BEHIND)
-        for gx in range(G - COPY_BEHIND, G):
-            copy_out(gx)
+            sums = psum.tile([PICKED, SLAB], F32)
+            nc.tensor.matmul(sums[:], weights[:], dens[:, slabs[gx]], start=True, stop=True)
+            nc.any.tensor_copy(staged[:, slabs[gx]], sums[:])
+            nc.sync.dma_start(out[:, slabs[gx]], staged[:, slabs[gx]])

import math

import concourse.mybir as mybir

F32 = mybir.dt.float32
BF16 = mybir.dt.bfloat16
U16 = mybir.dt.uint16
ALU = mybir.AluOpType
FN = mybir.ActivationFunctionType

ATOMS = 128
CHANNELS = 256
PICKED = 128
G = 16
SLAB = G * G
POINTS = G * SLAB
PSUM_BANKS = 8

GRID_ORIGIN = -3.75
GRID_STEP = 0.5
Q_CORE = 1.0
Q_END = 2.25
GAUSS_AT_END = math.exp(-2.0 * Q_END)

FLOPS = 2 * ATOMS * PICKED * POINTS


def tile_coords2grid_kernel(tc, coords, radii, types, offs, out):
    nc = tc.nc
    with (
        tc.tile_pool(name="held", bufs=1) as held,
        tc.psum_pool(name="psum", bufs=PSUM_BANKS) as psum,
    ):
        xyz = held.tile([ATOMS, 3], F32)
        nc.sync.dma_start(xyz[:], coords)
        radius = held.tile([ATOMS, 1], F32)
        nc.scalar.dma_start(radius[:], radii)
        offsets = held.tile([ATOMS, PICKED // 16], U16)
        nc.sync.dma_start(offsets[:], offs)
        table = held.tile([ATOMS, CHANNELS], F32)
        nc.scalar.dma_start(table[:], types)

        steps = held.tile([ATOMS, 3, G], F32)
        nc.gpsimd.iota(
            steps[:],
            pattern=[[0, 3], [1, G]],
            base=0,
            channel_multiplier=0,
            allow_small_or_imprecise_dtypes=True,
        )
        axis = held.tile([ATOMS, 3, G], F32)
        nc.gpsimd.tensor_scalar(axis[:], steps[:], GRID_STEP, GRID_ORIGIN, ALU.mult, ALU.add)

        two = held.tile([ATOMS, 1], F32)
        nc.vector.memset(two[:], 2.0)
        inv_gauss_at_core = held.tile([ATOMS, 1], F32)
        nc.scalar.activation(inv_gauss_at_core[:], two[:], FN.Exp, scale=Q_CORE)

        inv_radius = held.tile([ATOMS, 1], F32)
        nc.vector.reciprocal(inv_radius[:], radius[:])
        delta = held.tile([ATOMS, 3, G], F32)
        nc.vector.tensor_tensor(
            delta[:], axis[:], xyz[:].unsqueeze(2).to_broadcast([ATOMS, 3, G]), ALU.subtract
        )
        q_far = held.tile([ATOMS, 3, G], F32)
        nc.scalar.activation(q_far[:], delta[:], FN.Square, scale=inv_radius[:])

        gauss_axis = held.tile([ATOMS, 3, G], F32)
        nc.scalar.activation(gauss_axis[:], q_far[:], FN.Exp, scale=-2.0)
        root_x = held.tile([ATOMS, G], F32)
        nc.scalar.activation(root_x[:], q_far[:, 0, :], FN.Exp, scale=-1.0)

        picked = held.tile([ATOMS, PICKED], F32)
        nc.scalar.activation(picked[:], table[:].indirect(offsets[:]), FN.Copy)
        weights = held.tile([ATOMS, PICKED], BF16)
        nc.gpsimd.tensor_copy(weights[:], picked[:])

        q_axis = held.tile([ATOMS, 3, G], F32)
        nc.vector.tensor_scalar_min(q_axis[:], q_far[:], Q_END)
        q_x = q_axis[:, 0, :]
        q_yz = held.tile([ATOMS, SLAB], F32)
        nc.vector.tensor_tensor(
            q_yz[:].rearrange("n (y z) -> n y z", y=G),
            q_axis[:, 1, :].unsqueeze(2).to_broadcast([ATOMS, G, G]),
            q_axis[:, 2, :].unsqueeze(1).to_broadcast([ATOMS, G, G]),
            ALU.add,
        )
        low = held.tile([ATOMS, G], F32)
        nc.vector.tensor_scalar(low[:], q_x, -1.0, Q_CORE, ALU.mult, ALU.add)
        high = held.tile([ATOMS, G], F32)
        nc.vector.tensor_scalar(high[:], q_x, -1.0, Q_END, ALU.mult, ALU.add)

        tail_scale = held.tile([ATOMS, G], F32)
        nc.vector.tensor_scalar_mul(tail_scale[:], root_x[:], -2.0)
        tail_bias = held.tile([ATOMS, G], F32)
        nc.vector.tensor_scalar_mul(tail_bias[:], root_x[:], 3.0)
        inv_floor_x = held.tile([ATOMS, G], F32)
        nc.vector.tensor_scalar(
            inv_floor_x[:], gauss_axis[:, 0, :], GAUSS_AT_END, inv_gauss_at_core[:], ALU.max, ALU.mult
        )
        gauss_yz = held.tile([ATOMS, SLAB], F32)
        nc.vector.tensor_tensor(
            gauss_yz[:].rearrange("n (y z) -> n y z", y=G),
            gauss_axis[:, 1, :].unsqueeze(2).to_broadcast([ATOMS, G, G]),
            gauss_axis[:, 2, :].unsqueeze(1).to_broadcast([ATOMS, G, G]),
            ALU.mult,
        )
        floor_x = held.tile([ATOMS, G], F32)
        nc.vector.reciprocal(floor_x[:], inv_floor_x[:])

        q_clamped = held.tile([ATOMS, POINTS], F32)
        u_clamped = held.tile([ATOMS, POINTS], F32)
        tail = held.tile([ATOMS, POINTS], F32)
        dens = held.tile([ATOMS, POINTS], BF16)
        staged = held.tile([PICKED, POINTS], F32)
        slabs = [slice(gx * SLAB, (gx + 1) * SLAB) for gx in range(G)]

        for gx in range(G):
            nc.vector.tensor_scalar(
                q_clamped[:, slabs[gx]], q_yz[:], low[:, gx : gx + 1], high[:, gx : gx + 1], ALU.max, ALU.min
            )
            nc.scalar.activation(
                u_clamped[:, slabs[gx]], q_clamped[:, slabs[gx]], FN.Sqrt, bias=q_axis[:, 0, gx : gx + 1]
            )
            nc.scalar.activation(
                tail[:, slabs[gx]],
                u_clamped[:, slabs[gx]],
                FN.Square,
                bias=tail_bias[:, gx : gx + 1],
                scale=tail_scale[:, gx : gx + 1],
            )
            nc.vector.scalar_tensor_tensor(
                dens[:, slabs[gx]], gauss_yz[:], floor_x[:, gx : gx + 1], tail[:, slabs[gx]], op0=ALU.max, op1=ALU.mult
            )
            sums = psum.tile([PICKED, SLAB], F32)
            nc.tensor.matmul(sums[:], weights[:], dens[:, slabs[gx]], start=True, stop=True)
            nc.any.tensor_copy(staged[:, slabs[gx]], sums[:])
            nc.sync.dma_start(out[:, slabs[gx]], staged[:, slabs[gx]])
